import numpy as np
import ml_dtypes


def mxq(x, axis, fmt="e4m3"):
    dtype, down = {"e4m3": (ml_dtypes.float8_e4m3fn, 7), "e5m2": (ml_dtypes.float8_e5m2, 14)}[fmt]
    v = np.moveaxis(np.asarray(x, np.float32).astype(ml_dtypes.bfloat16).astype(np.float64), axis, -1)
    blocks = v.reshape(v.shape[:-1] + (-1, 32))
    amax = np.abs(blocks).max(-1, keepdims=True)
    byte = np.maximum(np.where(amax > 0, np.frexp(amax)[1] - 1 + 127, 0) - down, 1)
    scale = np.exp2(byte - 127.0)
    codes = (blocks / scale).astype(np.float32).astype(dtype).astype(np.float64)
    return np.moveaxis((codes * scale).reshape(v.shape), -1, axis)


WIDE = False


def mx_kscale(k):
    if not WIDE:
        return np.ones(k)
    levels = np.array([10, -10, 5, -5, 0])
    a = np.random.permutation(np.resize(levels, k // 512 * 4)).reshape(k // 512, 4)
    idx = np.arange(k)
    return np.exp2(a[idx // 512, idx % 128 // 32])


BF16 = ml_dtypes.bfloat16


def bf(x):
    return np.asarray(x, np.float32).astype(BF16)


def f64(x):
    return np.asarray(x).astype(np.float64)


B, SD, H, A = 8192, 512, 512, 128
MAX_ACTION = 1.0
LOG_SIG_MIN, LOG_SIG_MAX = -20.0, 2.0
EPS = 1e-6
LOG2PI = float(np.log(2.0 * np.pi))


def setup_inputs():
    s, t = mx_kscale(H), mx_kscale(H)
    h1 = np.maximum(np.random.standard_normal((B, H)), 0.0)
    bsig = 0.6 * np.random.standard_normal(A)
    bsig[np.random.permutation(A)[: A // 16]] -= 21.0
    return {"h1": bf(h1 * s),
            "W2": bf(np.random.standard_normal((H, H)) * np.sqrt(2.0 / H) / s[:, None] * t),
            "b2": bf(0.2 * np.random.standard_normal(H) * t),
            "Wmu": bf(np.random.standard_normal((H, A)) / np.sqrt(H) / t[:, None]),
            "bmu": bf(0.3 * np.random.standard_normal(A)),
            "Wsig": bf(1.4 * np.random.standard_normal((H, A)) / np.sqrt(H) / t[:, None]),
            "bsig": bf(bsig),
            "noise": bf(np.random.standard_normal((B, A)))}


def reference(h1, W2, b2, Wmu, bmu, Wsig, bsig, noise):
    h = np.maximum((mxq(f64(h1), 1, "e4m3") @ mxq(f64(W2), 0, "e4m3")) + f64(b2), 0.0)
    hq = mxq(h, 1, "e4m3")
    mu = (hq @ mxq(f64(Wmu), 0, "e4m3")) + f64(bmu)
    log_sigma = np.clip((hq @ mxq(f64(Wsig), 0, "e4m3")) + f64(bsig), LOG_SIG_MIN, LOG_SIG_MAX)
    sigma = np.exp(log_sigma)
    raw_actions = mu + sigma * f64(noise)
    z = (raw_actions - mu) / sigma
    log_pis = -0.5 * np.sum(z * z, axis=1) - np.sum(log_sigma, axis=1) - 0.5 * A * LOG2PI
    actions = np.tanh(raw_actions)
    log_pis = log_pis - np.sum(np.log(1.0 - actions * actions + EPS), axis=1)
    actions = actions * MAX_ACTION
    return actions, log_pis

@@ -1,0 +1,418 @@
+import math
+from contextlib import ExitStack
+
+import concourse.mybir as mybir
+from concourse.masks import make_identity
+
+F32 = mybir.dt.float32
+BF16 = mybir.dt.bfloat16
+U32 = mybir.dt.uint32
+U8 = mybir.dt.uint8
+FP8X4 = mybir.dt.float8_e4m3fn_x4
+ALU = mybir.AluOpType
+ACT = mybir.ActivationFunctionType
+AX = mybir.AxisListType
+
+P = 128
+B, H, A = 8192, 512, 128
+NT = B // P
+GT = 4
+GR = GT * P
+NG = NT // GT
+FLOPS = 2 * B * H * (H + 2 * A)
+
+N2_FILL = {0: 6, 1: 6, 2: 6, 3: 4}
+N2_DRAIN = 10
+N2_SG = 1
+
+
+def tile_gaussianactor_pa_kernel(tc, h1, W2, b2, Wmu, bmu, Wsig, bsig, noise, out_0, out_1):
+    nc = tc.nc
+    h1f = h1.rearrange("(p t) k -> p (t k)", t=NT)
+    nf = noise.rearrange("(p t) a -> p (t a)", t=NT)
+    af = out_0.rearrange("(p t) a -> p (t a)", t=NT)
+    lf = out_1.rearrange("(p t) -> p t", t=NT)
+
+    with ExitStack() as ctx:
+        keep = ctx.enter_context(tc.tile_pool(name="keep", bufs=1))
+        work = ctx.enter_context(tc.tile_pool(name="work", bufs=2))
+        psum = ctx.enter_context(tc.psum_pool(name="psum", bufs=1))
+        ctx.enter_context(tc.manual_schedule())
+        ctx.enter_context(nc.allow_non_contiguous_dma(reason="small bias vectors, one or four elements a partition"))
+
+        identf = keep.tile([P, P], F32, name="identf")
+        identb = keep.tile([P, P], BF16, name="identb")
+        W2r = keep.tile([P, 4 * H], BF16, name="W2r")
+        W2g = keep.tile([P, 4 * H], BF16, name="W2g", align_bytes=64)
+        W2c = keep.tile([P, H], U32, name="W2c", align_bytes=64)
+        W2s = keep.tile([P, H], U8, name="W2s", align_bytes=64)
+        Wr = keep.tile([P, 4 * 2 * A], BF16, name="Wr")
+        Wg = keep.tile([P, 4 * 2 * A], BF16, name="Wg", align_bytes=64)
+        Wc = keep.tile([P, 2 * A], U32, name="Wc", align_bytes=64)
+        Ws = keep.tile([P, 2 * A], U8, name="Ws", align_bytes=64)
+        b2b = keep.tile([P, 4], BF16, name="b2b")
+        b2f = keep.tile([P, 4], F32, name="b2f")
+        bmub = keep.tile([P, 1], BF16, name="bmub")
+        bmuf = keep.tile([P, 1], F32, name="bmuf")
+        bsb = keep.tile([P, 1], BF16, name="bsb")
+        bsf = keep.tile([P, 1], F32, name="bsf")
+        lo = keep.tile([P, 1], F32, name="lo")
+        hi = keep.tile([P, 1], F32, name="hi")
+        bsbc = keep.tile([P, A], BF16, name="bsbc")
+        bsum = keep.tile([P, 1], F32, name="bsum")
+        kp = keep.tile([P, 1], F32, name="kp")
+        eps = keep.tile([P, 1], F32, name="eps")
+        nz = keep.tile([P, NT * A], BF16, name="nz")
+        cT = keep.tile([P, B], F32, name="cT")
+        xT = keep.tile([P, B], F32, name="xT")
+        s1v = keep.tile([P, NT], F32, name="s1v")
+        s1s = keep.tile([P, NT], F32, name="s1s")
+        sc = keep.tile([P, NT], F32, name="sc")
+        s3 = keep.tile([P, NT], F32, name="s3")
+        base = keep.tile([P, NT], F32, name="base")
+        lp = keep.tile([P, NT], F32, name="lp")
+        junkv = keep.tile([P, A], F32, name="junkv")
+        junks = keep.tile([P, A], F32, name="junks")
+
+        st = {}
+        tp, h1g, h1c, h1s = {}, {}, {}, {}
+        s1, hT, hg, hc, hs = {}, {}, {}, {}, {}
+        sig, mu, sg, sn, nt = {}, {}, {}, {}, {}
+        xr, sp, sq_, aa, cr = {}, {}, {}, {}, {}
+        n2 = {"next": 0}
+
+        def ok(g):
+            return 0 <= g < NG
+
+        def load_h1(c, parts):
+            st[c] = work.tile([P, 2 * GT * H], BF16, name="st", tag="st", bufs=4)
+            w = 2 * GT * H // parts
+            for i in range(parts):
+                nc.sync.dma_start(
+                    out=st[c][:, i * w : (i + 1) * w],
+                    in_=h1f[:, c * 2 * GT * H + i * w : c * 2 * GT * H + (i + 1) * w],
+                )
+
+        def load_noise(c):
+            w = NT * A // 4
+            nc.sync.dma_start(out=nz[:, c * w : (c + 1) * w], in_=nf[:, c * w : (c + 1) * w])
+
+        def load_weights_first():
+            for u in range(2):
+                nc.scalar.dma_start(
+                    out=W2r[:, u * 2 * H : (u + 1) * 2 * H],
+                    in_=W2[u * 256 : (u + 1) * 256, :].rearrange("(q e) n -> q (e n)", e=2),
+                )
+            nc.scalar.dma_start(out=b2b[:], in_=b2.rearrange("(p m) -> p m", m=4))
+            make_identity(nc, identf[:])
+            make_identity(nc, identb[:])
+            nc.gpsimd.dma_start(out=bsb[:], in_=bsig.rearrange("(p o) -> p o", o=1))
+            nc.gpsimd.dma_start(out=bmub[:], in_=bmu.rearrange("(p o) -> p o", o=1))
+            nc.gpsimd.dma_start(out=bsbc[:], in_=bsig.partition_broadcast(P))
+
+        def load_weights_second():
+            wv = Wr[:].rearrange("p (j c) -> p j c", j=4)
+            nc.sync.dma_start(out=wv[:, :, 0:A], in_=Wmu.rearrange("(p j) a -> p j a", j=4))
+            nc.sync.dma_start(out=wv[:, :, A : 2 * A], in_=Wsig.rearrange("(p j) a -> p j a", j=4))
+
+        def prep_w2():
+            nc.vector.tensor_copy(
+                out=W2g[:].rearrange("q (m i t) -> q m i t", m=4, t=4),
+                in_=W2r[:].rearrange("q (t i m) -> q m i t", t=4, m=4),
+            )
+            nc.vector.tensor_copy(out=b2f[:], in_=b2b[:])
+            nc.vector.quantize_mx(out=W2c[:].bitcast(FP8X4), scales=W2s[:], in_=W2g[:])
+
+        def prep_small():
+            nc.vector.tensor_copy(out=bsf[:], in_=bsb[:])
+            nc.vector.tensor_copy(out=bmuf[:], in_=bmub[:])
+            nc.vector.tensor_scalar(out=lo[:], in0=bsf[:], scalar1=-1.0, scalar2=-20.0, op0=ALU.mult, op1=ALU.add)
+            nc.vector.tensor_scalar(out=hi[:], in0=bsf[:], scalar1=-1.0, scalar2=2.0, op0=ALU.mult, op1=ALU.add)
+            nc.vector.tensor_reduce(out=bsum[:], in_=bsbc[:], axis=AX.X, op=ALU.add)
+            nc.vector.tensor_scalar(
+                out=kp[:], in0=bsum[:], scalar1=1.0, scalar2=0.5 * A * math.log(2.0 * math.pi), op0=ALU.mult, op1=ALU.add
+            )
+
+        def prep_heads():
+            nc.vector.tensor_copy(
+                out=Wg[:].rearrange("p (c j) -> p c j", j=4),
+                in_=Wr[:].rearrange("p (j c) -> p c j", j=4),
+            )
+            nc.vector.quantize_mx(out=Wc[:].bitcast(FP8X4), scales=Ws[:], in_=Wg[:])
+
+        def T(g, b):
+            if not ok(g):
+                return
+            words = st[g // 2][:].bitcast(F32)
+            tp[g, b] = psum.tile([P, 512], F32, name="tp", tag="tp")
+            for jl in range(2):
+                j = (g % 2) * GT + 2 * b + jl
+                for u in range(2):
+                    nc.tensor.transpose(
+                        tp[g, b][:, (2 * jl + u) * P : (2 * jl + u + 1) * P],
+                        words[:, j * 256 + u * P : j * 256 + (u + 1) * P],
+                        identf[:],
+                    )
+
+        def X(g, b):
+            if not ok(g):
+                return
+            if b == 0:
+                h1g[g] = work.tile([P, 4 * GR], BF16, name="h1g", tag="h1g", align_bytes=64)
+            nc.scalar.copy(
+                out=h1g[g][:].bitcast(F32)[:, b * 512 : (b + 1) * 512].rearrange("p (j r u) -> p j r u", j=2, u=2),
+                in_=tp[g, b][:].rearrange("p (j u r) -> p j r u", j=2, u=2),
+            )
+
+        def Q1(g):
+            if not ok(g):
+                return
+            h1c[g] = work.tile([P, GR], U32, name="h1c", tag="h1c", align_bytes=64)
+            h1s[g] = work.tile([P, GR], U8, name="h1s", tag="h1s", align_bytes=64)
+            nc.vector.quantize_mx(out=h1c[g][:].bitcast(FP8X4), scales=h1s[g][:], in_=h1g[g][:])
+
+        def M1(g):
+            if not ok(g):
+                return
+            for m in range(4):
+                s1[g, m] = psum.tile([P, GR], F32, name="s1", tag="s1", bufs=4)
+                nc.tensor.matmul_mx(
+                    out=s1[g, m][:],
+                    lhsT=W2c[:, m * P : (m + 1) * P].bitcast(FP8X4),
+                    lhsT_scale=W2s[:, m * P : (m + 1) * P],
+                    rhs=h1c[g][:].bitcast(FP8X4),
+                    rhs_scale=h1s[g][:],
+                    start=True,
+                    stop=True,
+                )
+
+        def R(g, ms):
+            if not ok(g):
+                return
+            for m in ms:
+                if m == 0:
+                    hT[g] = work.tile([P, 4 * GR], BF16, name="hT", tag="hT")
+                nc.scalar.activation(
+                    out=hT[g][:, m * GR : (m + 1) * GR], in_=s1[g, m][:], func=ACT.Relu, bias=b2f[:, m : m + 1], scale=1.0
+                )
+
+        def RG(g):
+            if not ok(g):
+                return
+            hg[g] = work.tile([P, 4 * GR], BF16, name="hg", tag="hg", align_bytes=64)
+            nc.vector.tensor_copy(
+                out=hg[g][:].rearrange("p (c i t) -> p c t i", i=4, t=4),
+                in_=hT[g][:].rearrange("p (t c i) -> p c t i", t=4, i=4),
+            )
+
+        def Q2(g):
+            if not ok(g):
+                return
+            hc[g] = work.tile([P, GR], U32, name="hc", tag="hc", align_bytes=64)
+            hs[g] = work.tile([P, GR], U8, name="hs", tag="hs", align_bytes=64)
+            nc.vector.quantize_mx(out=hc[g][:].bitcast(FP8X4), scales=hs[g][:], in_=hg[g][:])
+
+        def M2(g, which):
+            if not ok(g):
+                return
+            t = psum.tile([P, GR], F32, name=which, tag=which)
+            c0 = 0 if which == "mu" else A
+            nc.tensor.matmul_mx(
+                out=t[:],
+                lhsT=Wc[:, c0 : c0 + A].bitcast(FP8X4),
+                lhsT_scale=Ws[:, c0 : c0 + A],
+                rhs=hc[g][:].bitcast(FP8X4),
+                rhs_scale=hs[g][:],
+                start=True,
+                stop=True,
+            )
+            if which == "mu":
+                mu[g] = t
+            else:
+                sig[g] = t
+
+        def C(g):
+            if not ok(g):
+                return
+            nc.vector.tensor_scalar(
+                out=cT[:, g * GR : (g + 1) * GR], in0=sig[g][:], scalar1=lo[:, 0:1], scalar2=hi[:, 0:1], op0=ALU.max, op1=ALU.min
+            )
+
+        def E(g):
+            if not ok(g):
+                return
+            sg[g] = work.tile([P, GR], F32, name="sg", tag="sg")
+            nc.scalar.activation(out=sg[g][:], in_=cT[:, g * GR : (g + 1) * GR], func=ACT.Exp, bias=bsf[:, 0:1], scale=1.0)
+
+        def NTR(k):
+            if not 0 <= k < NG // 2:
+                return
+            nt[k] = psum.tile([P, 2 * GR], BF16, name="nt", tag="nt")
+            for j in range(2 * GT):
+                t = k * 2 * GT + j
+                nc.tensor.transpose(nt[k][:, j * P : (j + 1) * P], nz[:, t * A : (t + 1) * A], identb[:])
+
+        def SN(g):
+            if not ok(g):
+                return
+            sn[g] = work.tile([P, GR], F32, name="sn", tag="sn")
+            nc.vector.tensor_tensor(
+                out=sn[g][:], in0=sg[g][:], in1=nt[g // 2][:, (g % 2) * GR : (g % 2 + 1) * GR], op=ALU.mult
+            )
+
+        def XX(g):
+            if not ok(g):
+                return
+            nc.vector.scalar_tensor_tensor(
+                out=xT[:, g * GR : (g + 1) * GR], in0=mu[g][:], scalar=bmuf[:, 0:1], in1=sn[g][:], op0=ALU.add, op1=ALU.add
+            )
+
+        def N2(eng, count):
+            for i in range(count):
+                t = n2["next"]
+                if t >= NT:
+                    return
+                n2["next"] = t + 1
+                src = nz[:, t * A : (t + 1) * A]
+                if eng == "S":
+                    nc.scalar.activation(
+                        out=junks[:], in_=src, func=ACT.Square, scale=math.sqrt(0.5), accum_out=s1s[:, t : t + 1]
+                    )
+                else:
+                    nc.vector.scalar_tensor_tensor(
+                        out=junkv[:], in0=src, scalar=0.5, in1=src, op0=ALU.mult, op1=ALU.mult, accum_out=s1v[:, t : t + 1]
+                    )
+
+        def XT(g):
+            xr[g] = psum.tile([P, GR], F32, name="xr", tag="s1", bufs=4)
+            for j in range(GT):
+                nc.tensor.transpose(
+                    xr[g][:, j * P : (j + 1) * P], xT[:, g * GR + j * P : g * GR + (j + 1) * P], identf[:]
+                )
+
+        def SG(g):
+            sp[g] = work.tile([P, GR], F32, name="sp", tag="sp", bufs=3)
+            sq_[g] = work.tile([P, GR], F32, name="sm", tag="sm", bufs=3)
+            nc.scalar.activation(out=sp[g][:], in_=xr[g][:], func=ACT.Sigmoid, scale=2.0)
+            nc.scalar.activation(out=sq_[g][:], in_=xr[g][:], func=ACT.Sigmoid, scale=-2.0)
+
+        def SQ(g):
+            if not ok(g):
+                return
+            nc.vector.tensor_tensor(out=xT[:, g * GR : (g + 1) * GR], in0=sp[g][:], in1=sq_[g][:], op=ALU.mult)
+
+        def AA(g):
+            if not ok(g):
+                return
+            aa[g] = work.tile([P, GR], F32, name="aa", tag="aa", bufs=3)
+            nc.vector.tensor_scalar(out=aa[g][:], in0=sp[g][:], scalar1=2.0, scalar2=-1.0, op0=ALU.mult, op1=ALU.add)
+            nc.sync.dma_start(out=af[:, g * GR : (g + 1) * GR], in_=aa[g][:])
+
+        def CT(g):
+            cr[g] = psum.tile([P, GR], F32, name="cr", tag=("tp", "nt", "sig", "mu")[g % 4])
+            for j in range(GT):
+                nc.tensor.transpose(
+                    cr[g][:, j * P : (j + 1) * P], cT[:, g * GR + j * P : g * GR + (j + 1) * P], identf[:]
+                )
+
+        def CR(g):
+            nc.vector.tensor_reduce(
+                out=sc[:, g * GT : (g + 1) * GT], in_=cr[g][:].rearrange("p (j a) -> p j a", j=GT), axis=AX.X, op=ALU.add
+            )
+
+        def LN(g):
+            for j in range(GT):
+                t = g * GT + j
+                nc.scalar.activation(
+                    out=junks[:],
+                    in_=xT[:, t * P : (t + 1) * P],
+                    func=ACT.Ln,
+                    bias=eps[:, 0:1],
+                    scale=4.0,
+                    accum_out=s3[:, t : t + 1],
+                )
+
+        load_weights_first()
+        load_h1(0, 2)
+        load_weights_second()
+        load_noise(0)
+        nc.vector.memset(eps[:], 1.0e-6)
+        nc.vector.memset(s1v[:], 0.0)
+        nc.vector.memset(s1s[:], 0.0)
+        prep_w2()
+        T(0, 0)
+        chunk = 1
+        for g in range(-1, NG):
+            if (g + 1) % 2 == 0 and chunk < NG // 2:
+                load_h1(chunk, 1)
+                if chunk < 4:
+                    load_noise(chunk)
+                chunk += 1
+            M1(g)
+            E(g - 3)
+            RG(g - 1)
+            X(g + 1, 0)
+            T(g + 1, 1)
+            C(g - 2)
+            R(g, (0, 1))
+            SN(g - 3)
+            if g == 1:
+                NTR(0)
+            if g >= 4 and g % 2 == 0:
+                NTR((g - 2) // 2)
+            XX(g - 3)
+            M2(g - 2, "mu")
+            N2("V", N2_FILL.get(g, 0))
+            X(g + 1, 1)
+            T(g + 2, 0)
+            Q2(g - 1)
+            M2(g - 1, "sig")
+            Q1(g + 1)
+            if g == -1:
+                prep_heads()
+            if g == 0:
+                prep_small()
+            R(g, (2, 3))
+        E(13)
+        RG(15)
+        C(14)
+        Q2(15)
+        M2(15, "sig")
+        E(14)
+        N2("S", N2_DRAIN)
+        SN(13)
+        C(15)
+        E(15)
+        XX(13)
+        M2(14, "mu")
+        NTR(7)
+        XT(0)
+        XT(1)
+        XT(2)
+        SN(14)
+        XX(14)
+        M2(15, "mu")
+        SN(15)
+        XX(15)
+        for g in range(NG):
+            if g >= 3:
+                XT(g)
+            SG(g)
+            SQ(g - 1)
+            AA(g - 1)
+            N2("V", N2_SG)
+        SQ(NG - 1)
+        AA(NG - 1)
+        for g in range(NG):
+            CT(g)
+            LN(g)
+            CR(g)
+            N2("V", 2)
+        N2("V", NT)
+        nc.vector.tensor_tensor(out=base[:], in0=s1v[:], in1=s1s[:], op=ALU.add)
+        nc.vector.tensor_tensor(out=base[:], in0=base[:], in1=sc[:], op=ALU.add)
+        nc.vector.tensor_scalar(out=base[:], in0=base[:], scalar1=kp[:, 0:1], scalar2=None, op0=ALU.add)
+        nc.vector.scalar_tensor_tensor(
+            out=lp[:], in0=base[:], scalar=-1.0, in1=s3[:], op0=ALU.mult, op1=ALU.subtract
+        )
+        nc.sync.dma_start(out=lf, in_=lp[:])

@@ -21,9 +21,10 @@ GR = GT * P
 NG = NT // GT
 FLOPS = 2 * B * H * (H + 2 * A)
 
-N2_FILL = {0: 6, 1: 6, 2: 6, 3: 4}
-N2_DRAIN = 10
+N2_FILL = {1: 4, 2: 6, 3: 6, 4: 4}
+N2_DRAIN = 12
 N2_SG = 1
+N2_LN = 1
 
 
 def tile_gaussianactor_pa_kernel(tc, h1, W2, b2, Wmu, bmu, Wsig, bsig, noise, out_0, out_1):
@@ -86,12 +87,14 @@ def tile_gaussianactor_pa_kernel(tc, h1, W2, b2, Wmu, bmu, Wsig, bsig, noise, ou
 
         def load_h1(c, parts):
             st[c] = work.tile([P, 2 * GT * H], BF16, name="st", tag="st", bufs=4)
-            w = 2 * GT * H // parts
-            for i in range(parts):
+            lo_col = 0
+            for tiles in parts:
+                hi_col = lo_col + tiles * H
                 nc.sync.dma_start(
-                    out=st[c][:, i * w : (i + 1) * w],
-                    in_=h1f[:, c * 2 * GT * H + i * w : c * 2 * GT * H + (i + 1) * w],
+                    out=st[c][:, lo_col:hi_col],
+                    in_=h1f[:, c * 2 * GT * H + lo_col : c * 2 * GT * H + hi_col],
                 )
+                lo_col = hi_col
 
         def load_noise(c):
             w = NT * A // 4
@@ -138,13 +141,14 @@ def tile_gaussianactor_pa_kernel(tc, h1, W2, b2, Wmu, bmu, Wsig, bsig, noise, ou
                 out=Wg[:].rearrange("p (c j) -> p c j", j=4),
                 in_=Wr[:].rearrange("p (j c) -> p c j", j=4),
             )
+            prep_small()
             nc.vector.quantize_mx(out=Wc[:].bitcast(FP8X4), scales=Ws[:], in_=Wg[:])
 
         def T(g, b):
             if not ok(g):
                 return
             words = st[g // 2][:].bitcast(F32)
-            tp[g, b] = psum.tile([P, 512], F32, name="tp", tag="tp")
+            tp[g, b] = psum.tile([P, 512], F32, name="tp", tag="tp", bufs=2)
             for jl in range(2):
                 j = (g % 2) * GT + 2 * b + jl
                 for u in range(2):
@@ -171,11 +175,11 @@ def tile_gaussianactor_pa_kernel(tc, h1, W2, b2, Wmu, bmu, Wsig, bsig, noise, ou
             h1s[g] = work.tile([P, GR], U8, name="h1s", tag="h1s", align_bytes=64)
             nc.vector.quantize_mx(out=h1c[g][:].bitcast(FP8X4), scales=h1s[g][:], in_=h1g[g][:])
 
-        def M1(g):
+        def M1(g, ms):
             if not ok(g):
                 return
-            for m in range(4):
-                s1[g, m] = psum.tile([P, GR], F32, name="s1", tag="s1", bufs=4)
+            for m in ms:
+                s1[g, m] = psum.tile([P, GR], F32, name="s1", tag="s1", bufs=3)
                 nc.tensor.matmul_mx(
                     out=s1[g, m][:],
                     lhsT=W2c[:, m * P : (m + 1) * P].bitcast(FP8X4),
@@ -208,8 +212,8 @@ def tile_gaussianactor_pa_kernel(tc, h1, W2, b2, Wmu, bmu, Wsig, bsig, noise, ou
         def Q2(g):
             if not ok(g):
                 return
-            hc[g] = work.tile([P, GR], U32, name="hc", tag="hc", align_bytes=64)
-            hs[g] = work.tile([P, GR], U8, name="hs", tag="hs", align_bytes=64)
+            hc[g] = work.tile([P, GR], U32, name="hc", tag="hc", bufs=3, align_bytes=64)
+            hs[g] = work.tile([P, GR], U8, name="hs", tag="hs", bufs=3, align_bytes=64)
             nc.vector.quantize_mx(out=hc[g][:].bitcast(FP8X4), scales=hs[g][:], in_=hg[g][:])
 
         def M2(g, which):
@@ -241,7 +245,7 @@ def tile_gaussianactor_pa_kernel(tc, h1, W2, b2, Wmu, bmu, Wsig, bsig, noise, ou
         def E(g):
             if not ok(g):
                 return
-            sg[g] = work.tile([P, GR], F32, name="sg", tag="sg")
+            sg[g] = work.tile([P, GR], F32, name="sg", tag="sg", bufs=4)
             nc.scalar.activation(out=sg[g][:], in_=cT[:, g * GR : (g + 1) * GR], func=ACT.Exp, bias=bsf[:, 0:1], scale=1.0)
 
         def NTR(k):
@@ -255,7 +259,7 @@ def tile_gaussianactor_pa_kernel(tc, h1, W2, b2, Wmu, bmu, Wsig, bsig, noise, ou
         def SN(g):
             if not ok(g):
                 return
-            sn[g] = work.tile([P, GR], F32, name="sn", tag="sn")
+            sn[g] = work.tile([P, GR], F32, name="sn", tag="sn", bufs=3)
             nc.vector.tensor_tensor(
                 out=sn[g][:], in0=sg[g][:], in1=nt[g // 2][:, (g % 2) * GR : (g % 2 + 1) * GR], op=ALU.mult
             )
@@ -284,7 +288,10 @@ def tile_gaussianactor_pa_kernel(tc, h1, W2, b2, Wmu, bmu, Wsig, bsig, noise, ou
                     )
 
         def XT(g):
-            xr[g] = psum.tile([P, GR], F32, name="xr", tag="s1", bufs=4)
+            if g % 5 < 3:
+                xr[g] = psum.tile([P, GR], F32, name="xr", tag="s1", bufs=3)
+            else:
+                xr[g] = psum.tile([P, GR], F32, name="xr", tag="tp", bufs=2)
             for j in range(GT):
                 nc.tensor.transpose(
                     xr[g][:, j * P : (j + 1) * P], xT[:, g * GR + j * P : g * GR + (j + 1) * P], identf[:]
@@ -309,7 +316,7 @@ def tile_gaussianactor_pa_kernel(tc, h1, W2, b2, Wmu, bmu, Wsig, bsig, noise, ou
             nc.sync.dma_start(out=af[:, g * GR : (g + 1) * GR], in_=aa[g][:])
 
         def CT(g):
-            cr[g] = psum.tile([P, GR], F32, name="cr", tag=("tp", "nt", "sig", "mu")[g % 4])
+            cr[g] = psum.tile([P, GR], F32, name="cr", tag=("nt", "sig", "mu")[g % 3])
             for j in range(GT):
                 nc.tensor.transpose(
                     cr[g][:, j * P : (j + 1) * P], cT[:, g * GR + j * P : g * GR + (j + 1) * P], identf[:]
@@ -333,7 +340,8 @@ def tile_gaussianactor_pa_kernel(tc, h1, W2, b2, Wmu, bmu, Wsig, bsig, noise, ou
                 )
 
         load_weights_first()
-        load_h1(0, 2)
+        load_h1(0, (2, 2, 4))
+        load_h1(1, (8,))
         load_weights_second()
         load_noise(0)
         nc.vector.memset(eps[:], 1.0e-6)
@@ -341,54 +349,65 @@ def tile_gaussianactor_pa_kernel(tc, h1, W2, b2, Wmu, bmu, Wsig, bsig, noise, ou
         nc.vector.memset(s1s[:], 0.0)
         prep_w2()
         T(0, 0)
+        T(0, 1)
         chunk = 1
-        for g in range(-1, NG):
-            if (g + 1) % 2 == 0 and chunk < NG // 2:
-                load_h1(chunk, 1)
+        for i in range(-1, NG + 1):
+            if (i + 1) % 2 == 0 and chunk < NG // 2:
+                if chunk > 1:
+                    load_h1(chunk, (8,))
                 if chunk < 4:
                     load_noise(chunk)
                 chunk += 1
-            M1(g)
-            E(g - 3)
-            RG(g - 1)
-            X(g + 1, 0)
-            T(g + 1, 1)
-            C(g - 2)
-            R(g, (0, 1))
-            SN(g - 3)
-            if g == 1:
+            SN(i - 5)
+            R(i - 1, (0,))
+            M1(i - 1, (3,))
+            M2(i - 3, "sig")
+            X(i + 1, 0)
+            RG(i - 2)
+            XX(i - 5)
+            R(i - 1, (1,))
+            M1(i, (0, 1, 2) if i == 0 else (0,))
+            X(i + 1, 1)
+            T(i + 2, 0)
+            T(i + 2, 1)
+            if i == 2:
                 NTR(0)
-            if g >= 4 and g % 2 == 0:
-                NTR((g - 2) // 2)
-            XX(g - 3)
-            M2(g - 2, "mu")
-            N2("V", N2_FILL.get(g, 0))
-            X(g + 1, 1)
-            T(g + 2, 0)
-            Q2(g - 1)
-            M2(g - 1, "sig")
-            Q1(g + 1)
-            if g == -1:
+            if i >= 6 and i % 2 == 0:
+                NTR((i - 4) // 2)
+            C(i - 3)
+            N2("V", N2_FILL.get(i, 0))
+            R(i - 1, (2,))
+            if i != 0:
+                M1(i, (1,))
+            M2(i - 4, "mu")
+            E(i - 4)
+            Q2(i - 2)
+            Q1(i + 1)
+            if i == 1:
                 prep_heads()
-            if g == 0:
-                prep_small()
-            R(g, (2, 3))
+            R(i - 1, (3,))
+            if i != 0:
+                M1(i, (2,))
+        M2(14, "sig")
         E(13)
         RG(15)
+        N2("S", N2_DRAIN)
         C(14)
+        E(14)
         Q2(15)
         M2(15, "sig")
-        E(14)
-        N2("S", N2_DRAIN)
-        SN(13)
+        SN(12)
         C(15)
         E(15)
-        XX(13)
-        M2(14, "mu")
-        NTR(7)
         XT(0)
         XT(1)
         XT(2)
+        XX(12)
+        M2(13, "mu")
+        SN(13)
+        NTR(7)
+        XX(13)
+        M2(14, "mu")
         SN(14)
         XX(14)
         M2(15, "mu")
@@ -407,7 +426,7 @@ def tile_gaussianactor_pa_kernel(tc, h1, W2, b2, Wmu, bmu, Wsig, bsig, noise, ou
             CT(g)
             LN(g)
             CR(g)
-            N2("V", 2)
+            N2("V", N2_LN)
         N2("V", NT)
         nc.vector.tensor_tensor(out=base[:], in0=s1v[:], in1=s1s[:], op=ALU.add)
         nc.vector.tensor_tensor(out=base[:], in0=base[:], in1=sc[:], op=ALU.add)

@@ -25,6 +25,7 @@ N2_FILL = {1: 4, 2: 6, 3: 6, 4: 4}
 N2_DRAIN = 12
 N2_SG = 1
 N2_LN = 1
+JS = 16
 
 
 def tile_gaussianactor_pa_kernel(tc, h1, W2, b2, Wmu, bmu, Wsig, bsig, noise, out_0, out_1):
@@ -72,8 +73,8 @@ def tile_gaussianactor_pa_kernel(tc, h1, W2, b2, Wmu, bmu, Wsig, bsig, noise, ou
         s3 = keep.tile([P, NT], F32, name="s3")
         base = keep.tile([P, NT], F32, name="base")
         lp = keep.tile([P, NT], F32, name="lp")
-        junkv = keep.tile([P, A], F32, name="junkv")
-        junks = keep.tile([P, A], F32, name="junks")
+        junkv = keep.tile([P, JS * A], F32, name="junkv")
+        junks = keep.tile([P, JS * A], F32, name="junks")
 
         st = {}
         tp, h1g, h1c, h1s = {}, {}, {}, {}
@@ -280,11 +281,11 @@ def tile_gaussianactor_pa_kernel(tc, h1, W2, b2, Wmu, bmu, Wsig, bsig, noise, ou
                 src = nz[:, t * A : (t + 1) * A]
                 if eng == "S":
                     nc.scalar.activation(
-                        out=junks[:], in_=src, func=ACT.Square, scale=math.sqrt(0.5), accum_out=s1s[:, t : t + 1]
+                        out=junks[:, (t % JS) * A : (t % JS + 1) * A], in_=src, func=ACT.Square, scale=math.sqrt(0.5), accum_out=s1s[:, t : t + 1]
                     )
                 else:
                     nc.vector.scalar_tensor_tensor(
-                        out=junkv[:], in0=src, scalar=0.5, in1=src, op0=ALU.mult, op1=ALU.mult, accum_out=s1v[:, t : t + 1]
+                        out=junkv[:, (t % JS) * A : (t % JS + 1) * A], in0=src, scalar=0.5, in1=src, op0=ALU.mult, op1=ALU.mult, accum_out=s1v[:, t : t + 1]
                     )
 
         def XT(g):
@@ -331,7 +332,7 @@ def tile_gaussianactor_pa_kernel(tc, h1, W2, b2, Wmu, bmu, Wsig, bsig, noise, ou
             for j in range(GT):
                 t = g * GT + j
                 nc.scalar.activation(
-                    out=junks[:],
+                    out=junks[:, (t % JS) * A : (t % JS + 1) * A],
                     in_=xT[:, t * P : (t + 1) * P],
                     func=ACT.Ln,
                     bias=eps[:, 0:1],

@@ -58,18 +58,11 @@ def tile_gaussianactor_pa_kernel(tc, h1, W2, b2, Wmu, bmu, Wsig, bsig, noise, ou
         bmuf = keep.tile([P, 1], F32, name="bmuf")
         bsb = keep.tile([P, 1], BF16, name="bsb")
         bsf = keep.tile([P, 1], F32, name="bsf")
-        lo = keep.tile([P, 1], F32, name="lo")
-        hi = keep.tile([P, 1], F32, name="hi")
-        bsbc = keep.tile([P, A], BF16, name="bsbc")
-        bsum = keep.tile([P, 1], F32, name="bsum")
-        kp = keep.tile([P, 1], F32, name="kp")
-        eps = keep.tile([P, 1], F32, name="eps")
         nz = keep.tile([P, NT * A], BF16, name="nz")
-        cT = keep.tile([P, B], F32, name="cT")
+        sT = keep.tile([P, B], F32, name="sT")
         xT = keep.tile([P, B], F32, name="xT")
         s1v = keep.tile([P, NT], F32, name="s1v")
         s1s = keep.tile([P, NT], F32, name="s1s")
-        sc = keep.tile([P, NT], F32, name="sc")
         s3 = keep.tile([P, NT], F32, name="s3")
         base = keep.tile([P, NT], F32, name="base")
         lp = keep.tile([P, NT], F32, name="lp")
@@ -112,7 +105,6 @@ def tile_gaussianactor_pa_kernel(tc, h1, W2, b2, Wmu, bmu, Wsig, bsig, noise, ou
             make_identity(nc, identb[:])
             nc.gpsimd.dma_start(out=bsb[:], in_=bsig.rearrange("(p o) -> p o", o=1))
             nc.gpsimd.dma_start(out=bmub[:], in_=bmu.rearrange("(p o) -> p o", o=1))
-            nc.gpsimd.dma_start(out=bsbc[:], in_=bsig.partition_broadcast(P))
 
         def load_weights_second():
             wv = Wr[:].rearrange("p (j c) -> p j c", j=4)
@@ -130,12 +122,6 @@ def tile_gaussianactor_pa_kernel(tc, h1, W2, b2, Wmu, bmu, Wsig, bsig, noise, ou
         def prep_small():
             nc.vector.tensor_copy(out=bsf[:], in_=bsb[:])
             nc.vector.tensor_copy(out=bmuf[:], in_=bmub[:])
-            nc.vector.tensor_scalar(out=lo[:], in0=bsf[:], scalar1=-1.0, scalar2=-20.0, op0=ALU.mult, op1=ALU.add)
-            nc.vector.tensor_scalar(out=hi[:], in0=bsf[:], scalar1=-1.0, scalar2=2.0, op0=ALU.mult, op1=ALU.add)
-            nc.vector.tensor_reduce(out=bsum[:], in_=bsbc[:], axis=AX.X, op=ALU.add)
-            nc.vector.tensor_scalar(
-                out=kp[:], in0=bsum[:], scalar1=1.0, scalar2=0.5 * A * math.log(2.0 * math.pi), op0=ALU.mult, op1=ALU.add
-            )
 
         def prep_heads():
             nc.vector.tensor_copy(
@@ -236,18 +222,23 @@ def tile_gaussianactor_pa_kernel(tc, h1, W2, b2, Wmu, bmu, Wsig, bsig, noise, ou
             else:
                 sig[g] = t
 
-        def C(g):
-            if not ok(g):
-                return
-            nc.vector.tensor_scalar(
-                out=cT[:, g * GR : (g + 1) * GR], in0=sig[g][:], scalar1=lo[:, 0:1], scalar2=hi[:, 0:1], op0=ALU.max, op1=ALU.min
-            )
-
         def E(g):
             if not ok(g):
                 return
             sg[g] = work.tile([P, GR], F32, name="sg", tag="sg", bufs=4)
-            nc.scalar.activation(out=sg[g][:], in_=cT[:, g * GR : (g + 1) * GR], func=ACT.Exp, bias=bsf[:, 0:1], scale=1.0)
+            nc.scalar.activation(out=sg[g][:], in_=sig[g][:], func=ACT.Exp, bias=bsf[:, 0:1], scale=1.0)
+
+        def C(g):
+            if not ok(g):
+                return
+            nc.vector.tensor_scalar(
+                out=sT[:, g * GR : (g + 1) * GR],
+                in0=sg[g][:],
+                scalar1=math.exp(-20.0),
+                scalar2=math.exp(2.0),
+                op0=ALU.max,
+                op1=ALU.min,
+            )
 
         def NTR(k):
             if not 0 <= k < NG // 2:
@@ -262,7 +253,7 @@ def tile_gaussianactor_pa_kernel(tc, h1, W2, b2, Wmu, bmu, Wsig, bsig, noise, ou
                 return
             sn[g] = work.tile([P, GR], F32, name="sn", tag="sn", bufs=3)
             nc.vector.tensor_tensor(
-                out=sn[g][:], in0=sg[g][:], in1=nt[g // 2][:, (g % 2) * GR : (g % 2 + 1) * GR], op=ALU.mult
+                out=sn[g][:], in0=sT[:, g * GR : (g + 1) * GR], in1=nt[g // 2][:, (g % 2) * GR : (g % 2 + 1) * GR], op=ALU.mult
             )
 
         def XX(g):
@@ -317,15 +308,24 @@ def tile_gaussianactor_pa_kernel(tc, h1, W2, b2, Wmu, bmu, Wsig, bsig, noise, ou
             nc.sync.dma_start(out=af[:, g * GR : (g + 1) * GR], in_=aa[g][:])
 
         def CT(g):
+            if not ok(g):
+                return
             cr[g] = psum.tile([P, GR], F32, name="cr", tag=("nt", "sig", "mu")[g % 3])
             for j in range(GT):
                 nc.tensor.transpose(
-                    cr[g][:, j * P : (j + 1) * P], cT[:, g * GR + j * P : g * GR + (j + 1) * P], identf[:]
+                    cr[g][:, j * P : (j + 1) * P], sT[:, g * GR + j * P : g * GR + (j + 1) * P], identf[:]
                 )
 
         def CR(g):
-            nc.vector.tensor_reduce(
-                out=sc[:, g * GT : (g + 1) * GT], in_=cr[g][:].rearrange("p (j a) -> p j a", j=GT), axis=AX.X, op=ALU.add
+            if not ok(g):
+                return
+            nc.vector.scalar_tensor_tensor(
+                out=sT[:, g * GR : (g + 1) * GR],
+                in0=xT[:, g * GR : (g + 1) * GR],
+                scalar=0.25e-6,
+                in1=cr[g][:],
+                op0=ALU.add,
+                op1=ALU.mult,
             )
 
         def LN(g):
@@ -333,9 +333,8 @@ def tile_gaussianactor_pa_kernel(tc, h1, W2, b2, Wmu, bmu, Wsig, bsig, noise, ou
                 t = g * GT + j
                 nc.scalar.activation(
                     out=junks[:, (t % JS) * A : (t % JS + 1) * A],
-                    in_=xT[:, t * P : (t + 1) * P],
+                    in_=sT[:, t * P : (t + 1) * P],
                     func=ACT.Ln,
-                    bias=eps[:, 0:1],
                     scale=4.0,
                     accum_out=s3[:, t : t + 1],
                 )
@@ -345,7 +344,6 @@ def tile_gaussianactor_pa_kernel(tc, h1, W2, b2, Wmu, bmu, Wsig, bsig, noise, ou
         load_h1(1, (8,))
         load_weights_second()
         load_noise(0)
-        nc.vector.memset(eps[:], 1.0e-6)
         nc.vector.memset(s1v[:], 0.0)
         nc.vector.memset(s1s[:], 0.0)
         prep_w2()
@@ -375,13 +373,13 @@ def tile_gaussianactor_pa_kernel(tc, h1, W2, b2, Wmu, bmu, Wsig, bsig, noise, ou
                 NTR(0)
             if i >= 6 and i % 2 == 0:
                 NTR((i - 4) // 2)
-            C(i - 3)
+            C(i - 4)
             N2("V", N2_FILL.get(i, 0))
             R(i - 1, (2,))
             if i != 0:
                 M1(i, (1,))
             M2(i - 4, "mu")
-            E(i - 4)
+            E(i - 3)
             Q2(i - 2)
             Q1(i + 1)
             if i == 1:
@@ -390,15 +388,14 @@ def tile_gaussianactor_pa_kernel(tc, h1, W2, b2, Wmu, bmu, Wsig, bsig, noise, ou
             if i != 0:
                 M1(i, (2,))
         M2(14, "sig")
-        E(13)
         RG(15)
-        N2("S", N2_DRAIN)
-        C(14)
         E(14)
+        N2("S", N2_DRAIN)
+        C(13)
         Q2(15)
         M2(15, "sig")
         SN(12)
-        C(15)
+        C(14)
         E(15)
         XT(0)
         XT(1)
@@ -407,31 +404,38 @@ def tile_gaussianactor_pa_kernel(tc, h1, W2, b2, Wmu, bmu, Wsig, bsig, noise, ou
         M2(13, "mu")
         SN(13)
         NTR(7)
+        C(15)
         XX(13)
         M2(14, "mu")
         SN(14)
+        N2("V", 1)
         XX(14)
         M2(15, "mu")
         SN(15)
+        N2("V", 1)
         XX(15)
         for g in range(NG):
             if g >= 3:
                 XT(g)
+            if g >= NG - 3:
+                CT(g - (NG - 3))
             SG(g)
             SQ(g - 1)
             AA(g - 1)
             N2("V", N2_SG)
         SQ(NG - 1)
+        CR(0)
         AA(NG - 1)
+        CR(1)
         for g in range(NG):
-            CT(g)
+            CT(g + 3)
             LN(g)
-            CR(g)
+            CR(g + 2)
             N2("V", N2_LN)
         N2("V", NT)
-        nc.vector.tensor_tensor(out=base[:], in0=s1v[:], in1=s1s[:], op=ALU.add)
-        nc.vector.tensor_tensor(out=base[:], in0=base[:], in1=sc[:], op=ALU.add)
-        nc.vector.tensor_scalar(out=base[:], in0=base[:], scalar1=kp[:, 0:1], scalar2=None, op0=ALU.add)
+        nc.vector.scalar_tensor_tensor(
+            out=base[:], in0=s1v[:], scalar=0.5 * A * math.log(2.0 * math.pi), in1=s1s[:], op0=ALU.add, op1=ALU.add
+        )
         nc.vector.scalar_tensor_tensor(
             out=lp[:], in0=base[:], scalar=-1.0, in1=s3[:], op0=ALU.mult, op1=ALU.subtract
         )

@@ -23,7 +23,7 @@ FLOPS = 2 * B * H * (H + 2 * A)
 
 N2_FILL = {1: 4, 2: 6, 3: 6, 4: 4}
 N2_DRAIN = 12
-N2_SG = 1
+N2_SG = 2
 N2_LN = 1
 JS = 16
 
@@ -64,6 +64,7 @@ def tile_gaussianactor_pa_kernel(tc, h1, W2, b2, Wmu, bmu, Wsig, bsig, noise, ou
         s1v = keep.tile([P, NT], F32, name="s1v")
         s1s = keep.tile([P, NT], F32, name="s1s")
         s3 = keep.tile([P, NT], F32, name="s3")
+        gate = keep.tile([P, 1], F32, name="gate")
         base = keep.tile([P, NT], F32, name="base")
         lp = keep.tile([P, NT], F32, name="lp")
         junkv = keep.tile([P, JS * A], F32, name="junkv")
@@ -74,6 +75,7 @@ def tile_gaussianactor_pa_kernel(tc, h1, W2, b2, Wmu, bmu, Wsig, bsig, noise, ou
         s1, hT, hg, hc, hs = {}, {}, {}, {}, {}
         sig, mu, sg, sn, nt = {}, {}, {}, {}, {}
         xr, sp, sq_, aa, cr = {}, {}, {}, {}, {}
+        sp4 = {}
         n2 = {"next": 0}
 
         def ok(g):
@@ -290,21 +292,23 @@ def tile_gaussianactor_pa_kernel(tc, h1, W2, b2, Wmu, bmu, Wsig, bsig, noise, ou
                 )
 
         def SG(g):
-            sp[g] = work.tile([P, GR], F32, name="sp", tag="sp", bufs=3)
+            if g % 4 == 0:
+                sp4[g // 4] = work.tile([P, 2 * GT * H], BF16, name="sp4", tag="st", bufs=4)
+            sp[g] = sp4[g // 4][:].bitcast(F32)[:, (g % 4) * GR : (g % 4 + 1) * GR]
             sq_[g] = work.tile([P, GR], F32, name="sm", tag="sm", bufs=3)
-            nc.scalar.activation(out=sp[g][:], in_=xr[g][:], func=ACT.Sigmoid, scale=2.0)
+            nc.scalar.activation(out=sp[g], in_=xr[g][:], func=ACT.Sigmoid, scale=2.0)
             nc.scalar.activation(out=sq_[g][:], in_=xr[g][:], func=ACT.Sigmoid, scale=-2.0)
 
         def SQ(g):
             if not ok(g):
                 return
-            nc.vector.tensor_tensor(out=xT[:, g * GR : (g + 1) * GR], in0=sp[g][:], in1=sq_[g][:], op=ALU.mult)
+            nc.vector.tensor_tensor(out=xT[:, g * GR : (g + 1) * GR], in0=sp[g], in1=sq_[g][:], op=ALU.mult)
 
         def AA(g):
             if not ok(g):
                 return
-            aa[g] = work.tile([P, GR], F32, name="aa", tag="aa", bufs=3)
-            nc.vector.tensor_scalar(out=aa[g][:], in0=sp[g][:], scalar1=2.0, scalar2=-1.0, op0=ALU.mult, op1=ALU.add)
+            aa[g] = work.tile([P, GR], F32, name="aa", tag="aa", bufs=6)
+            nc.gpsimd.tensor_scalar(out=aa[g][:], in0=sp[g], scalar1=2.0, scalar2=-1.0, op0=ALU.mult, op1=ALU.add)
             nc.sync.dma_start(out=af[:, g * GR : (g + 1) * GR], in_=aa[g][:])
 
         def CT(g):
@@ -421,17 +425,16 @@ def tile_gaussianactor_pa_kernel(tc, h1, W2, b2, Wmu, bmu, Wsig, bsig, noise, ou
                 CT(g - (NG - 3))
             SG(g)
             SQ(g - 1)
-            AA(g - 1)
             N2("V", N2_SG)
         SQ(NG - 1)
+        nc.gpsimd.tensor_copy(out=gate[:], in_=xT[:, B - 1 : B])
         CR(0)
-        AA(NG - 1)
         CR(1)
         for g in range(NG):
             CT(g + 3)
             LN(g)
             CR(g + 2)
-            N2("V", N2_LN)
+            AA(g)
         N2("V", NT)
         nc.vector.scalar_tensor_tensor(
             out=base[:], in0=s1v[:], scalar=0.5 * A * math.log(2.0 * math.pi), in1=s1s[:], op0=ALU.add, op1=ALU.add

@@ -76,6 +76,7 @@ def tile_gaussianactor_pa_kernel(tc, h1, W2, b2, Wmu, bmu, Wsig, bsig, noise, ou
         sig, mu, sg, sn, nt = {}, {}, {}, {}, {}
         xr, sp, sq_, aa, cr = {}, {}, {}, {}, {}
         sp4 = {}
+        qin, qc, qs = {}, {}, {}
         n2 = {"next": 0}
 
         def ok(g):
@@ -150,19 +151,26 @@ def tile_gaussianactor_pa_kernel(tc, h1, W2, b2, Wmu, bmu, Wsig, bsig, noise, ou
         def X(g, b):
             if not ok(g):
                 return
-            if b == 0:
-                h1g[g] = work.tile([P, 4 * GR], BF16, name="h1g", tag="h1g", align_bytes=64)
             nc.scalar.copy(
-                out=h1g[g][:].bitcast(F32)[:, b * 512 : (b + 1) * 512].rearrange("p (j r u) -> p j r u", j=2, u=2),
+                out=qtile(g - 1)[:].bitcast(F32)[:, 2 * GR + b * 512 : 2 * GR + (b + 1) * 512].rearrange("p (j r u) -> p j r u", j=2, u=2),
                 in_=tp[g, b][:].rearrange("p (j u r) -> p j r u", j=2, u=2),
             )
 
-        def Q1(g):
-            if not ok(g):
+        def qtile(i):
+            if i not in qin:
+                qin[i] = work.tile([P, 8 * GR], BF16, name="qin", tag="qin", bufs=2, align_bytes=64)
+            return qin[i]
+
+        def Q(i):
+            lo_c = 0 if ok(i - 2) else GR
+            hi_c = 2 * GR if ok(i + 1) else GR
+            if lo_c >= hi_c:
                 return
-            h1c[g] = work.tile([P, GR], U32, name="h1c", tag="h1c", align_bytes=64)
-            h1s[g] = work.tile([P, GR], U8, name="h1s", tag="h1s", align_bytes=64)
-            nc.vector.quantize_mx(out=h1c[g][:].bitcast(FP8X4), scales=h1s[g][:], in_=h1g[g][:])
+            qc[i] = work.tile([P, 2 * GR], U32, name="qc", tag="qc", bufs=4, align_bytes=64)
+            qs[i] = work.tile([P, 2 * GR], U8, name="qs", tag="qs", bufs=4, align_bytes=64)
+            nc.vector.quantize_mx(
+                out=qc[i][:, lo_c:hi_c].bitcast(FP8X4), scales=qs[i][:, lo_c:hi_c], in_=qtile(i)[:, 4 * lo_c : 4 * hi_c]
+            )
 
         def M1(g, ms):
             if not ok(g):
@@ -173,8 +181,8 @@ def tile_gaussianactor_pa_kernel(tc, h1, W2, b2, Wmu, bmu, Wsig, bsig, noise, ou
                     out=s1[g, m][:],
                     lhsT=W2c[:, m * P : (m + 1) * P].bitcast(FP8X4),
                     lhsT_scale=W2s[:, m * P : (m + 1) * P],
-                    rhs=h1c[g][:].bitcast(FP8X4),
-                    rhs_scale=h1s[g][:],
+                    rhs=qc[g - 1][:, GR : 2 * GR].bitcast(FP8X4),
+                    rhs_scale=qs[g - 1][:, GR : 2 * GR],
                     start=True,
                     stop=True,
                 )
@@ -192,18 +200,10 @@ def tile_gaussianactor_pa_kernel(tc, h1, W2, b2, Wmu, bmu, Wsig, bsig, noise, ou
         def RG(g):
             if not ok(g):
                 return
-            hg[g] = work.tile([P, 4 * GR], BF16, name="hg", tag="hg", align_bytes=64)
             nc.vector.tensor_copy(
-                out=hg[g][:].rearrange("p (c i t) -> p c t i", i=4, t=4),
+                out=qtile(g + 2)[:, 0 : 4 * GR].rearrange("p (c i t) -> p c t i", i=4, t=4),
                 in_=hT[g][:].rearrange("p (t c i) -> p c t i", t=4, i=4),
             )
-
-        def Q2(g):
-            if not ok(g):
-                return
-            hc[g] = work.tile([P, GR], U32, name="hc", tag="hc", bufs=3, align_bytes=64)
-            hs[g] = work.tile([P, GR], U8, name="hs", tag="hs", bufs=3, align_bytes=64)
-            nc.vector.quantize_mx(out=hc[g][:].bitcast(FP8X4), scales=hs[g][:], in_=hg[g][:])
 
         def M2(g, which):
             if not ok(g):
@@ -214,8 +214,8 @@ def tile_gaussianactor_pa_kernel(tc, h1, W2, b2, Wmu, bmu, Wsig, bsig, noise, ou
                 out=t[:],
                 lhsT=Wc[:, c0 : c0 + A].bitcast(FP8X4),
                 lhsT_scale=Ws[:, c0 : c0 + A],
-                rhs=hc[g][:].bitcast(FP8X4),
-                rhs_scale=hs[g][:],
+                rhs=qc[g + 2][:, 0:GR].bitcast(FP8X4),
+                rhs_scale=qs[g + 2][:, 0:GR],
                 start=True,
                 stop=True,
             )
@@ -384,8 +384,7 @@ def tile_gaussianactor_pa_kernel(tc, h1, W2, b2, Wmu, bmu, Wsig, bsig, noise, ou
                 M1(i, (1,))
             M2(i - 4, "mu")
             E(i - 3)
-            Q2(i - 2)
-            Q1(i + 1)
+            Q(i)
             if i == 1:
                 prep_heads()
             R(i - 1, (3,))
@@ -396,7 +395,7 @@ def tile_gaussianactor_pa_kernel(tc, h1, W2, b2, Wmu, bmu, Wsig, bsig, noise, ou
         E(14)
         N2("S", N2_DRAIN)
         C(13)
-        Q2(15)
+        Q(17)
         M2(15, "sig")
         SN(12)
         C(14)

@@ -61,13 +61,14 @@ def tile_gaussianactor_pa_kernel(tc, h1, W2, b2, Wmu, bmu, Wsig, bsig, noise, ou
         nz = keep.tile([P, NT * A], BF16, name="nz")
         sT = keep.tile([P, B], F32, name="sT")
         xT = keep.tile([P, B], F32, name="xT")
+        st6 = keep.tile([P, NT * 6], F32, name="st6")
+        sqm = keep.tile([P, NT * 2], F32, name="sqm")
         s1v = keep.tile([P, NT], F32, name="s1v")
         s1s = keep.tile([P, NT], F32, name="s1s")
         s3 = keep.tile([P, NT], F32, name="s3")
         gate = keep.tile([P, 1], F32, name="gate")
         base = keep.tile([P, NT], F32, name="base")
         lp = keep.tile([P, NT], F32, name="lp")
-        junkv = keep.tile([P, JS * A], F32, name="junkv")
         junks = keep.tile([P, JS * A], F32, name="junks")
 
         st = {}
@@ -277,9 +278,7 @@ def tile_gaussianactor_pa_kernel(tc, h1, W2, b2, Wmu, bmu, Wsig, bsig, noise, ou
                         out=junks[:, (t % JS) * A : (t % JS + 1) * A], in_=src, func=ACT.Square, scale=math.sqrt(0.5), accum_out=s1s[:, t : t + 1]
                     )
                 else:
-                    nc.vector.scalar_tensor_tensor(
-                        out=junkv[:, (t % JS) * A : (t % JS + 1) * A], in0=src, scalar=0.5, in1=src, op0=ALU.mult, op1=ALU.mult, accum_out=s1v[:, t : t + 1]
-                    )
+                    nc.vector.bn_stats(out=st6[:, t * 6 : (t + 1) * 6], in_=src)
 
         def XT(g):
             if g % 5 < 3:
@@ -307,7 +306,7 @@ def tile_gaussianactor_pa_kernel(tc, h1, W2, b2, Wmu, bmu, Wsig, bsig, noise, ou
         def AA(g):
             if not ok(g):
                 return
-            aa[g] = work.tile([P, GR], F32, name="aa", tag="aa", bufs=6)
+            aa[g] = work.tile([P, GR], F32, name="aa", tag="aa", bufs=8)
             nc.gpsimd.tensor_scalar(out=aa[g][:], in0=sp[g], scalar1=2.0, scalar2=-1.0, op0=ALU.mult, op1=ALU.add)
             nc.sync.dma_start(out=af[:, g * GR : (g + 1) * GR], in_=aa[g][:])
 
@@ -348,7 +347,7 @@ def tile_gaussianactor_pa_kernel(tc, h1, W2, b2, Wmu, bmu, Wsig, bsig, noise, ou
         load_h1(1, (8,))
         load_weights_second()
         load_noise(0)
-        nc.vector.memset(s1v[:], 0.0)
+        nc.vector.memset(st6[:], 0.0)
         nc.vector.memset(s1s[:], 0.0)
         prep_w2()
         T(0, 0)
@@ -429,15 +428,27 @@ def tile_gaussianactor_pa_kernel(tc, h1, W2, b2, Wmu, bmu, Wsig, bsig, noise, ou
         nc.gpsimd.tensor_copy(out=gate[:], in_=xT[:, B - 1 : B])
         CR(0)
         CR(1)
+        v6 = st6[:].rearrange("p (t s k) -> p t s k", s=2, k=3)
+        sq3 = sqm[:].rearrange("p (t s o) -> p t s o", s=2, o=1)
         for g in range(NG):
             CT(g + 3)
             LN(g)
             CR(g + 2)
             AA(g)
-        N2("V", NT)
-        nc.vector.scalar_tensor_tensor(
-            out=base[:], in0=s1v[:], scalar=0.5 * A * math.log(2.0 * math.pi), in1=s1s[:], op0=ALU.add, op1=ALU.add
-        )
+            if g == 1:
+                nc.vector.tensor_tensor(out=sq3, in0=v6[:, :, :, 1:2], in1=v6[:, :, :, 1:2], op=ALU.mult)
+            if g == 2:
+                nc.vector.scalar_tensor_tensor(
+                    out=sq3, in0=sq3, scalar=0.5 * A, in1=v6[:, :, :, 2:3], op0=ALU.mult, op1=ALU.add
+                )
+            if g == 3:
+                nc.vector.tensor_reduce(out=s1v[:], in_=sqm[:].rearrange("p (t s) -> p t s", s=2), axis=AX.X, op=ALU.add)
+            if g == 4:
+                nc.vector.tensor_scalar(
+                    out=s1v[:], in0=s1v[:], scalar1=0.5, scalar2=0.5 * A * math.log(2.0 * math.pi), op0=ALU.mult, op1=ALU.add
+                )
+            if g == 5:
+                nc.vector.tensor_tensor(out=base[:], in0=s1v[:], in1=s1s[:], op=ALU.add)
         nc.vector.scalar_tensor_tensor(
             out=lp[:], in0=base[:], scalar=-1.0, in1=s3[:], op0=ALU.mult, op1=ALU.subtract
         )

import math
from contextlib import ExitStack

import concourse.mybir as mybir
from concourse.masks import make_identity

F32 = mybir.dt.float32
BF16 = mybir.dt.bfloat16
U32 = mybir.dt.uint32
U8 = mybir.dt.uint8
FP8X4 = mybir.dt.float8_e4m3fn_x4
ALU = mybir.AluOpType
ACT = mybir.ActivationFunctionType
AX = mybir.AxisListType

P = 128
B, H, A = 8192, 512, 128
NT = B // P
GT = 4
GR = GT * P
NG = NT // GT
FLOPS = 2 * B * H * (H + 2 * A)

N2_FILL = {1: 4, 2: 6, 3: 6, 4: 4}
N2_DRAIN = 12
N2_SG = 2
N2_LN = 1
JS = 16


def tile_gaussianactor_pa_kernel(tc, h1, W2, b2, Wmu, bmu, Wsig, bsig, noise, out_0, out_1):
    nc = tc.nc
    h1f = h1.rearrange("(p t) k -> p (t k)", t=NT)
    nf = noise.rearrange("(p t) a -> p (t a)", t=NT)
    af = out_0.rearrange("(p t) a -> p (t a)", t=NT)
    lf = out_1.rearrange("(p t) -> p t", t=NT)

    with ExitStack() as ctx:
        keep = ctx.enter_context(tc.tile_pool(name="keep", bufs=1))
        work = ctx.enter_context(tc.tile_pool(name="work", bufs=2))
        psum = ctx.enter_context(tc.psum_pool(name="psum", bufs=1))
        ctx.enter_context(tc.manual_schedule())
        ctx.enter_context(nc.allow_non_contiguous_dma(reason="small bias vectors, one or four elements a partition"))

        identf = keep.tile([P, P], F32, name="identf")
        identb = keep.tile([P, P], BF16, name="identb")
        W2r = keep.tile([P, 4 * H], BF16, name="W2r")
        W2g = keep.tile([P, 4 * H], BF16, name="W2g", align_bytes=64)
        W2c = keep.tile([P, H], U32, name="W2c", align_bytes=64)
        W2s = keep.tile([P, H], U8, name="W2s", align_bytes=64)
        Wr = keep.tile([P, 4 * 2 * A], BF16, name="Wr")
        Wg = keep.tile([P, 4 * 2 * A], BF16, name="Wg", align_bytes=64)
        Wc = keep.tile([P, 2 * A], U32, name="Wc", align_bytes=64)
        Ws = keep.tile([P, 2 * A], U8, name="Ws", align_bytes=64)
        b2b = keep.tile([P, 4], BF16, name="b2b")
        b2f = keep.tile([P, 4], F32, name="b2f")
        bmub = keep.tile([P, 1], BF16, name="bmub")
        bmuf = keep.tile([P, 1], F32, name="bmuf")
        bsb = keep.tile([P, 1], BF16, name="bsb")
        bsf = keep.tile([P, 1], F32, name="bsf")
        nz = keep.tile([P, NT * A], BF16, name="nz")
        sT = keep.tile([P, B], F32, name="sT")
        xT = keep.tile([P, B], F32, name="xT")
        st6 = keep.tile([P, NT * 6], F32, name="st6")
        sqm = keep.tile([P, NT * 2], F32, name="sqm")
        s1v = keep.tile([P, NT], F32, name="s1v")
        s1s = keep.tile([P, NT], F32, name="s1s")
        s3 = keep.tile([P, NT], F32, name="s3")
        gate = keep.tile([P, 1], F32, name="gate")
        base = keep.tile([P, NT], F32, name="base")
        lp = keep.tile([P, NT], F32, name="lp")
        junks = keep.tile([P, JS * A], F32, name="junks")

        st = {}
        tp, h1g, h1c, h1s = {}, {}, {}, {}
        s1, hT, hg, hc, hs = {}, {}, {}, {}, {}
        sig, mu, sg, sn, nt = {}, {}, {}, {}, {}
        xr, sp, sq_, aa, cr = {}, {}, {}, {}, {}
        sp4 = {}
        qin, qc, qs = {}, {}, {}
        n2 = {"next": 0}

        def ok(g):
            return 0 <= g < NG

        def load_h1(c, parts):
            st[c] = work.tile([P, 2 * GT * H], BF16, name="st", tag="st", bufs=4)
            lo_col = 0
            for tiles in parts:
                hi_col = lo_col + tiles * H
                nc.sync.dma_start(
                    out=st[c][:, lo_col:hi_col],
                    in_=h1f[:, c * 2 * GT * H + lo_col : c * 2 * GT * H + hi_col],
                )
                lo_col = hi_col

        def load_noise(c):
            w = NT * A // 4
            nc.sync.dma_start(out=nz[:, c * w : (c + 1) * w], in_=nf[:, c * w : (c + 1) * w])

        def load_weights_first():
            for u in range(2):
                nc.scalar.dma_start(
                    out=W2r[:, u * 2 * H : (u + 1) * 2 * H],
                    in_=W2[u * 256 : (u + 1) * 256, :].rearrange("(q e) n -> q (e n)", e=2),
                )
            nc.scalar.dma_start(out=b2b[:], in_=b2.rearrange("(p m) -> p m", m=4))
            make_identity(nc, identf[:])
            make_identity(nc, identb[:])
            nc.gpsimd.dma_start(out=bsb[:], in_=bsig.rearrange("(p o) -> p o", o=1))
            nc.gpsimd.dma_start(out=bmub[:], in_=bmu.rearrange("(p o) -> p o", o=1))

        def load_weights_second():
            wv = Wr[:].rearrange("p (j c) -> p j c", j=4)
            nc.sync.dma_start(out=wv[:, :, 0:A], in_=Wmu.rearrange("(p j) a -> p j a", j=4))
            nc.sync.dma_start(out=wv[:, :, A : 2 * A], in_=Wsig.rearrange("(p j) a -> p j a", j=4))

        def prep_w2():
            nc.vector.tensor_copy(
                out=W2g[:].rearrange("q (m i t) -> q m i t", m=4, t=4),
                in_=W2r[:].rearrange("q (t i m) -> q m i t", t=4, m=4),
            )
            nc.vector.tensor_copy(out=b2f[:], in_=b2b[:])
            nc.vector.quantize_mx(out=W2c[:].bitcast(FP8X4), scales=W2s[:], in_=W2g[:])

        def prep_small():
            nc.vector.tensor_copy(out=bsf[:], in_=bsb[:])
            nc.vector.tensor_copy(out=bmuf[:], in_=bmub[:])

        def prep_heads():
            nc.vector.tensor_copy(
                out=Wg[:].rearrange("p (c j) -> p c j", j=4),
                in_=Wr[:].rearrange("p (j c) -> p c j", j=4),
            )
            prep_small()
            nc.vector.quantize_mx(out=Wc[:].bitcast(FP8X4), scales=Ws[:], in_=Wg[:])

        def T(g, b):
            if not ok(g):
                return
            words = st[g // 2][:].bitcast(F32)
            tp[g, b] = psum.tile([P, 512], F32, name="tp", tag="tp", bufs=2)
            for jl in range(2):
                j = (g % 2) * GT + 2 * b + jl
                for u in range(2):
                    nc.tensor.transpose(
                        tp[g, b][:, (2 * jl + u) * P : (2 * jl + u + 1) * P],
                        words[:, j * 256 + u * P : j * 256 + (u + 1) * P],
                        identf[:],
                    )

        def X(g, b):
            if not ok(g):
                return
            nc.scalar.copy(
                out=qtile(g - 1)[:].bitcast(F32)[:, 2 * GR + b * 512 : 2 * GR + (b + 1) * 512].rearrange("p (j r u) -> p j r u", j=2, u=2),
                in_=tp[g, b][:].rearrange("p (j u r) -> p j r u", j=2, u=2),
            )

        def qtile(i):
            if i not in qin:
                qin[i] = work.tile([P, 8 * GR], BF16, name="qin", tag="qin", bufs=2, align_bytes=64)
            return qin[i]

        def Q(i):
            lo_c = 0 if ok(i - 2) else GR
            hi_c = 2 * GR if ok(i + 1) else GR
            if lo_c >= hi_c:
                return
            qc[i] = work.tile([P, 2 * GR], U32, name="qc", tag="qc", bufs=4, align_bytes=64)
            qs[i] = work.tile([P, 2 * GR], U8, name="qs", tag="qs", bufs=4, align_bytes=64)
            nc.vector.quantize_mx(
                out=qc[i][:, lo_c:hi_c].bitcast(FP8X4), scales=qs[i][:, lo_c:hi_c], in_=qtile(i)[:, 4 * lo_c : 4 * hi_c]
            )

        def M1(g, ms):
            if not ok(g):
                return
            for m in ms:
                s1[g, m] = psum.tile([P, GR], F32, name="s1", tag="s1", bufs=3)
                nc.tensor.matmul_mx(
                    out=s1[g, m][:],
                    lhsT=W2c[:, m * P : (m + 1) * P].bitcast(FP8X4),
                    lhsT_scale=W2s[:, m * P : (m + 1) * P],
                    rhs=qc[g - 1][:, GR : 2 * GR].bitcast(FP8X4),
                    rhs_scale=qs[g - 1][:, GR : 2 * GR],
                    start=True,
                    stop=True,
                )

        def R(g, ms):
            if not ok(g):
                return
            for m in ms:
                if m == 0:
                    hT[g] = work.tile([P, 4 * GR], BF16, name="hT", tag="hT")
                nc.scalar.activation(
                    out=hT[g][:, m * GR : (m + 1) * GR], in_=s1[g, m][:], func=ACT.Relu, bias=b2f[:, m : m + 1], scale=1.0
                )

        def RG(g):
            if not ok(g):
                return
            nc.vector.tensor_copy(
                out=qtile(g + 2)[:, 0 : 4 * GR].rearrange("p (c i t) -> p c t i", i=4, t=4),
                in_=hT[g][:].rearrange("p (t c i) -> p c t i", t=4, i=4),
            )

        def M2(g, which):
            if not ok(g):
                return
            t = psum.tile([P, GR], F32, name=which, tag=which)
            c0 = 0 if which == "mu" else A
            nc.tensor.matmul_mx(
                out=t[:],
                lhsT=Wc[:, c0 : c0 + A].bitcast(FP8X4),
                lhsT_scale=Ws[:, c0 : c0 + A],
                rhs=qc[g + 2][:, 0:GR].bitcast(FP8X4),
                rhs_scale=qs[g + 2][:, 0:GR],
                start=True,
                stop=True,
            )
            if which == "mu":
                mu[g] = t
            else:
                sig[g] = t

        def E(g):
            if not ok(g):
                return
            sg[g] = work.tile([P, GR], F32, name="sg", tag="sg", bufs=4)
            nc.scalar.activation(out=sg[g][:], in_=sig[g][:], func=ACT.Exp, bias=bsf[:, 0:1], scale=1.0)

        def C(g):
            if not ok(g):
                return
            nc.vector.tensor_scalar(
                out=sT[:, g * GR : (g + 1) * GR],
                in0=sg[g][:],
                scalar1=math.exp(-20.0),
                scalar2=math.exp(2.0),
                op0=ALU.max,
                op1=ALU.min,
            )

        def NTR(k):
            if not 0 <= k < NG // 2:
                return
            nt[k] = psum.tile([P, 2 * GR], BF16, name="nt", tag="nt")
            for j in range(2 * GT):
                t = k * 2 * GT + j
                nc.tensor.transpose(nt[k][:, j * P : (j + 1) * P], nz[:, t * A : (t + 1) * A], identb[:])

        def SN(g):
            if not ok(g):
                return
            sn[g] = work.tile([P, GR], F32, name="sn", tag="sn", bufs=3)
            nc.vector.tensor_tensor(
                out=sn[g][:], in0=sT[:, g * GR : (g + 1) * GR], in1=nt[g // 2][:, (g % 2) * GR : (g % 2 + 1) * GR], op=ALU.mult
            )

        def XX(g):
            if not ok(g):
                return
            nc.vector.scalar_tensor_tensor(
                out=xT[:, g * GR : (g + 1) * GR], in0=mu[g][:], scalar=bmuf[:, 0:1], in1=sn[g][:], op0=ALU.add, op1=ALU.add
            )

        def N2(eng, count):
            for i in range(count):
                t = n2["next"]
                if t >= NT:
                    return
                n2["next"] = t + 1
                src = nz[:, t * A : (t + 1) * A]
                if eng == "S":
                    nc.scalar.activation(
                        out=junks[:, (t % JS) * A : (t % JS + 1) * A], in_=src, func=ACT.Square, scale=math.sqrt(0.5), accum_out=s1s[:, t : t + 1]
                    )
                else:
                    nc.vector.bn_stats(out=st6[:, t * 6 : (t + 1) * 6], in_=src)

        def XT(g):
            if g % 5 < 3:
                xr[g] = psum.tile([P, GR], F32, name="xr", tag="s1", bufs=3)
            else:
                xr[g] = psum.tile([P, GR], F32, name="xr", tag="tp", bufs=2)
            for j in range(GT):
                nc.tensor.transpose(
                    xr[g][:, j * P : (j + 1) * P], xT[:, g * GR + j * P : g * GR + (j + 1) * P], identf[:]
                )

        def SG(g):
            if g % 4 == 0:
                sp4[g // 4] = work.tile([P, 2 * GT * H], BF16, name="sp4", tag="st", bufs=4)
            sp[g] = sp4[g // 4][:].bitcast(F32)[:, (g % 4) * GR : (g % 4 + 1) * GR]
            sq_[g] = work.tile([P, GR], F32, name="sm", tag="sm", bufs=3)
            nc.scalar.activation(out=sp[g], in_=xr[g][:], func=ACT.Sigmoid, scale=2.0)
            nc.scalar.activation(out=sq_[g][:], in_=xr[g][:], func=ACT.Sigmoid, scale=-2.0)

        def SQ(g):
            if not ok(g):
                return
            nc.vector.tensor_tensor(out=xT[:, g * GR : (g + 1) * GR], in0=sp[g], in1=sq_[g][:], op=ALU.mult)

        def AA(g):
            if not ok(g):
                return
            aa[g] = work.tile([P, GR], F32, name="aa", tag="aa", bufs=8)
            nc.gpsimd.tensor_scalar(out=aa[g][:], in0=sp[g], scalar1=2.0, scalar2=-1.0, op0=ALU.mult, op1=ALU.add)
            nc.sync.dma_start(out=af[:, g * GR : (g + 1) * GR], in_=aa[g][:])

        def CT(g):
            if not ok(g):
                return
            cr[g] = psum.tile([P, GR], F32, name="cr", tag=("nt", "sig", "mu")[g % 3])
            for j in range(GT):
                nc.tensor.transpose(
                    cr[g][:, j * P : (j + 1) * P], sT[:, g * GR + j * P : g * GR + (j + 1) * P], identf[:]
                )

        def CR(g):
            if not ok(g):
                return
            nc.vector.scalar_tensor_tensor(
                out=sT[:, g * GR : (g + 1) * GR],
                in0=xT[:, g * GR : (g + 1) * GR],
                scalar=0.25e-6,
                in1=cr[g][:],
                op0=ALU.add,
                op1=ALU.mult,
            )

        def LN(g):
            for j in range(GT):
                t = g * GT + j
                nc.scalar.activation(
                    out=junks[:, (t % JS) * A : (t % JS + 1) * A],
                    in_=sT[:, t * P : (t + 1) * P],
                    func=ACT.Ln,
                    scale=4.0,
                    accum_out=s3[:, t : t + 1],
                )

        load_weights_first()
        load_h1(0, (2, 2, 4))
        load_h1(1, (8,))
        load_weights_second()
        load_noise(0)
        nc.vector.memset(st6[:], 0.0)
        nc.vector.memset(s1s[:], 0.0)
        prep_w2()
        T(0, 0)
        T(0, 1)
        chunk = 1
        for i in range(-1, NG + 1):
            if (i + 1) % 2 == 0 and chunk < NG // 2:
                if chunk > 1:
                    load_h1(chunk, (8,))
                if chunk < 4:
                    load_noise(chunk)
                chunk += 1
            SN(i - 5)
            R(i - 1, (0,))
            M1(i - 1, (3,))
            M2(i - 3, "sig")
            X(i + 1, 0)
            RG(i - 2)
            XX(i - 5)
            R(i - 1, (1,))
            M1(i, (0, 1, 2) if i == 0 else (0,))
            X(i + 1, 1)
            T(i + 2, 0)
            T(i + 2, 1)
            if i == 2:
                NTR(0)
            if i >= 6 and i % 2 == 0:
                NTR((i - 4) // 2)
            C(i - 4)
            N2("V", N2_FILL.get(i, 0))
            R(i - 1, (2,))
            if i != 0:
                M1(i, (1,))
            M2(i - 4, "mu")
            E(i - 3)
            Q(i)
            if i == 1:
                prep_heads()
            R(i - 1, (3,))
            if i != 0:
                M1(i, (2,))
        M2(14, "sig")
        RG(15)
        E(14)
        N2("S", N2_DRAIN)
        C(13)
        Q(17)
        M2(15, "sig")
        SN(12)
        C(14)
        E(15)
        XT(0)
        XT(1)
        XT(2)
        XX(12)
        M2(13, "mu")
        SN(13)
        NTR(7)
        C(15)
        XX(13)
        M2(14, "mu")
        SN(14)
        N2("V", 1)
        XX(14)
        M2(15, "mu")
        SN(15)
        N2("V", 1)
        XX(15)
        for g in range(NG):
            if g >= 3:
                XT(g)
            if g >= NG - 3:
                CT(g - (NG - 3))
            SG(g)
            SQ(g - 1)
            N2("V", N2_SG)
        SQ(NG - 1)
        nc.gpsimd.tensor_copy(out=gate[:], in_=xT[:, B - 1 : B])
        CR(0)
        CR(1)
        v6 = st6[:].rearrange("p (t s k) -> p t s k", s=2, k=3)
        sq3 = sqm[:].rearrange("p (t s o) -> p t s o", s=2, o=1)
        for g in range(NG):
            CT(g + 3)
            LN(g)
            CR(g + 2)
            AA(g)
            if g == 1:
                nc.vector.tensor_tensor(out=sq3, in0=v6[:, :, :, 1:2], in1=v6[:, :, :, 1:2], op=ALU.mult)
            if g == 2:
                nc.vector.scalar_tensor_tensor(
                    out=sq3, in0=sq3, scalar=0.5 * A, in1=v6[:, :, :, 2:3], op0=ALU.mult, op1=ALU.add
                )
            if g == 3:
                nc.vector.tensor_reduce(out=s1v[:], in_=sqm[:].rearrange("p (t s) -> p t s", s=2), axis=AX.X, op=ALU.add)
            if g == 4:
                nc.vector.tensor_scalar(
                    out=s1v[:], in0=s1v[:], scalar1=0.5, scalar2=0.5 * A * math.log(2.0 * math.pi), op0=ALU.mult, op1=ALU.add
                )
            if g == 5:
                nc.vector.tensor_tensor(out=base[:], in0=s1v[:], in1=s1s[:], op=ALU.add)
        nc.vector.scalar_tensor_tensor(
            out=lp[:], in0=base[:], scalar=-1.0, in1=s3[:], op0=ALU.mult, op1=ALU.subtract
        )
        nc.sync.dma_start(out=lf, in_=lp[:])
